import numpy as np
import ml_dtypes


def mxq(x, axis, fmt="e4m3"):
    dtype, down = {"e4m3": (ml_dtypes.float8_e4m3fn, 7), "e5m2": (ml_dtypes.float8_e5m2, 14)}[fmt]
    v = np.moveaxis(np.asarray(x, np.float32).astype(ml_dtypes.bfloat16).astype(np.float64), axis, -1)
    blocks = v.reshape(v.shape[:-1] + (-1, 32))
    amax = np.abs(blocks).max(-1, keepdims=True)
    byte = np.maximum(np.where(amax > 0, np.frexp(amax)[1] - 1 + 127, 0) - down, 1)
    scale = np.exp2(byte - 127.0)
    codes = (blocks / scale).astype(np.float32).astype(dtype).astype(np.float64)
    return np.moveaxis((codes * scale).reshape(v.shape), -1, axis)


WIDE = False


def mx_kscale(k):
    if not WIDE:
        return np.ones(k)
    levels = np.array([10, -10, 5, -5, 0])
    a = np.random.permutation(np.resize(levels, k // 512 * 4)).reshape(k // 512, 4)
    idx = np.arange(k)
    return np.exp2(a[idx // 512, idx % 128 // 32])


BF16 = ml_dtypes.bfloat16


def bf(x):
    return np.asarray(x, np.float32).astype(BF16)


def f64(x):
    return np.asarray(x).astype(np.float64)


B, T, C, H, NOPE, ROPE, VD, LORA = 4, 1024, 1024, 4, 128, 128, 128, 512
QK = NOPE + ROPE
HALF = ROPE // 2


def make_freq_cis():
    inv = 1.0 / (10000.0 ** (np.arange(0, ROPE, 2) / ROPE))
    ang = np.outer(np.arange(T), inv)
    return np.stack([np.cos(ang), np.sin(ang)], -1)


def apply_rope(v, fc):
    vr = v.reshape(B, T, H, HALF, 2)
    f = fc.reshape(1, T, 1, HALF, 2)
    real = vr[..., 0] * f[..., 0] - vr[..., 1] * f[..., 1]
    imag = vr[..., 1] * f[..., 0] + vr[..., 0] * f[..., 1]
    return np.stack([real, imag], -1).reshape(B, T, H, ROPE)


def setup_inputs():
    s = mx_kscale(C)
    return {"x": bf(np.random.standard_normal((B, T, C)) * s),
            "freq_cis": bf(make_freq_cis()),
            "Wq": bf(np.random.standard_normal((C, H * QK)) * 2.0 / np.sqrt(C) / s[:, None])}


def reference(x, freq_cis, Wq):
    q = (mxq(f64(x), 2, "e4m3") @ mxq(f64(Wq), 0, "e4m3")).reshape(B, T, H, QK)
    q_nope, q_rope = q[..., :NOPE], q[..., NOPE:]
    q_rope = apply_rope(q_rope, f64(freq_cis))
    return np.concatenate([q_nope, q_rope], -1)

@@ -1,0 +1,246 @@
+from contextlib import ExitStack
+
+import concourse.mybir as mybir
+from concourse.masks import make_identity
+
+F32 = mybir.dt.float32
+BF16 = mybir.dt.bfloat16
+U32 = mybir.dt.uint32
+U8 = mybir.dt.uint8
+FP8X4 = mybir.dt.float8_e4m3fn_x4
+MULT = mybir.AluOpType.mult
+ADD = mybir.AluOpType.add
+
+P = 128
+PACK = 4
+K_PASS = P * PACK
+TOKENS = 4 * 1024
+POSITIONS = 1024
+K = 1024
+PASSES = K // K_PASS
+HEADS = 4
+HALF_HEAD = 128
+PAIRS = HALF_HEAD // 2
+FEATURES = HEADS * 2 * HALF_HEAD
+BANK = HEADS * HALF_HEAD
+KEPT = 0
+ROTATED = 1
+ROUND_TILES = 2
+ROUND_TOKENS = ROUND_TILES * P
+ROUNDS = TOKENS // ROUND_TOKENS
+POSITION_ROUNDS = POSITIONS // ROUND_TOKENS
+AHEAD = 2
+RUN = 4
+
+FLOPS = 2 * TOKENS * K * FEATURES
+
+
+def tile_multiheadlatentattention_pb_t_kernel(tc, x, freq_cis, Wq, out):
+    nc = tc.nc
+    x_rounds = x.rearrange("b t k -> (b t) k").rearrange(
+        "(r p a) k -> r p (a k)", p=P, a=ROUND_TILES
+    )
+    out_rounds = out.rearrange("b t h f -> (b t) (h f)").rearrange(
+        "(r p a) f -> r p (a f)", p=P, a=ROUND_TILES
+    )
+
+    with ExitStack() as ctx:
+        keep = ctx.enter_context(tc.tile_pool(name="keep", bufs=1))
+        x_pool = ctx.enter_context(tc.tile_pool(name="x_pool", bufs=ROUNDS))
+        grouped_pool = ctx.enter_context(tc.tile_pool(name="grouped_pool", bufs=3))
+        codes_pool = ctx.enter_context(tc.tile_pool(name="codes_pool", bufs=AHEAD + 2))
+        out_pool = ctx.enter_context(tc.tile_pool(name="out_pool", bufs=4))
+        cross_pool = ctx.enter_context(tc.tile_pool(name="cross_pool", bufs=4))
+        xt_psum = ctx.enter_context(tc.psum_pool(name="xt_psum", bufs=ROUND_TILES))
+        kept_psum = ctx.enter_context(tc.psum_pool(name="kept_psum", bufs=3))
+        rotated_psum = ctx.enter_context(tc.psum_pool(name="rotated_psum", bufs=3))
+        ctx.enter_context(tc.manual_schedule())
+
+        w_raw = []
+        for g in range(PASSES):
+            w_rows = keep.tile([P, PACK * FEATURES], BF16, name="w_raw%d" % g)
+            nc.sync.dma_start(
+                out=w_rows[:].rearrange("q (u c) -> q u c", u=2),
+                in_=Wq[g * K_PASS : (g + 1) * K_PASS, :].rearrange(
+                    "(u q e) c -> q u (e c)", u=2, e=2
+                ),
+            )
+            w_raw.append(w_rows)
+        table = keep.tile([P, POSITION_ROUNDS * ROUND_TILES * PAIRS * 2], BF16, name="table")
+        x_tiles = []
+        for r in range(ROUNDS):
+            x_sb = x_pool.tile([P, ROUND_TILES * K], BF16, name="x_sb")
+            nc.sync.dma_start(out=x_sb[:], in_=x_rounds[r])
+            x_tiles.append(x_sb)
+            if r == 0:
+                nc.sync.dma_start(
+                    out=table[:].rearrange("p (r c) -> p r c", r=POSITION_ROUNDS),
+                    in_=freq_cis.rearrange(
+                        "(r p a) i two -> p r (a i two)", p=P, a=ROUND_TILES
+                    ),
+                )
+
+        identity = keep.tile([P, P], F32, name="identity")
+        make_identity(nc, identity[:])
+
+        w_codes = {}
+        w_scales = {}
+        w_grouped = {}
+        for g in range(PASSES):
+            for kind in (KEPT, ROTATED):
+                grouped = keep.tile(
+                    [P, BANK * PACK], BF16, name="w_grouped%d%d" % (g, kind), align_bytes=64
+                )
+                w_grouped[g, kind] = grouped
+                for h in range(HEADS):
+                    rows = w_raw[g][:].rearrange(
+                        "q (t h kind c i) -> q h kind c t i", t=PACK, h=HEADS, kind=2, i=RUN
+                    )[:, h, kind]
+                    words = grouped[:].rearrange(
+                        "q (h c i t) -> q h c t i", h=HEADS, i=RUN, t=PACK
+                    )[:, h]
+                    if h < HEADS // 2:
+                        nc.vector.tensor_copy(out=words, in_=rows)
+                    else:
+                        nc.scalar.copy(out=words, in_=rows)
+        for g in range(PASSES):
+            for kind in (KEPT, ROTATED):
+                w_codes[g, kind] = keep.tile(
+                    [P, BANK], U32, name="w_codes%d%d" % (g, kind), align_bytes=64
+                )
+                w_scales[g, kind] = keep.tile(
+                    [P, BANK], U8, name="w_scales%d%d" % (g, kind), align_bytes=64
+                )
+                nc.vector.quantize_mx(
+                    out=w_codes[g, kind][:].bitcast(FP8X4),
+                    scales=w_scales[g, kind][:],
+                    in_=w_grouped[g, kind][:],
+                )
+
+        xt_banks = {}
+        x_grouped = {}
+        x_codes = {}
+        x_scales = {}
+
+        def transpose(r):
+            words = x_tiles[r][:].bitcast(F32)
+            for a in range(ROUND_TILES):
+                xt = xt_psum.tile([P, PASSES * 2 * P], F32, name="xt")
+                for j in range(PASSES * 2):
+                    first = (a * PASSES * 2 + j) * P
+                    nc.tensor.transpose(
+                        xt[:, j * P : (j + 1) * P], words[:, first : first + P], identity[:]
+                    )
+                xt_banks[r, a] = xt
+
+        def copy_out(r):
+            grouped = grouped_pool.tile(
+                [P, ROUND_TILES * PASSES * P * PACK], BF16, name="x_grouped", align_bytes=64
+            )
+            pairs = grouped[:].bitcast(F32).rearrange(
+                "q (a g n u) -> q a g n u", a=ROUND_TILES, g=PASSES, u=2
+            )
+            for a in range(ROUND_TILES):
+                nc.scalar.copy(
+                    out=pairs[:, a],
+                    in_=xt_banks[r, a][:].rearrange("q (g u n) -> q g n u", g=PASSES, u=2),
+                )
+            x_grouped[r] = grouped
+
+        def quantise(r):
+            x_codes[r] = codes_pool.tile(
+                [P, ROUND_TILES * PASSES * P], U32, name="x_codes", align_bytes=64
+            )
+            x_scales[r] = codes_pool.tile(
+                [P, ROUND_TILES * PASSES * P], U8, name="x_scales", align_bytes=64
+            )
+            nc.vector.quantize_mx(
+                out=x_codes[r][:].bitcast(FP8X4), scales=x_scales[r][:], in_=x_grouped[r][:]
+            )
+
+        def multiply(r):
+            banks = {}
+            for a in range(ROUND_TILES):
+                banks[a, KEPT] = kept_psum.tile([P, BANK], F32, name="kept")
+                banks[a, ROTATED] = rotated_psum.tile([P, BANK], F32, name="rotated")
+                for kind in (KEPT, ROTATED):
+                    for g in range(PASSES):
+                        tokens = slice((a * PASSES + g) * P, (a * PASSES + g + 1) * P)
+                        nc.tensor.matmul_mx(
+                            out=banks[a, kind][:],
+                            lhsT=x_codes[r][:, tokens].bitcast(FP8X4),
+                            lhsT_scale=x_scales[r][:, tokens],
+                            rhs=w_codes[g, kind][:].bitcast(FP8X4),
+                            rhs_scale=w_scales[g, kind][:],
+                            start=(g == 0),
+                            stop=(g == PASSES - 1),
+                        )
+            return banks
+
+        def finish(r, banks):
+            out_sb = out_pool.tile([P, ROUND_TILES * FEATURES], F32, name="out_sb")
+            heads = out_sb[:].rearrange(
+                "p (a h kind f) -> p a h kind f", a=ROUND_TILES, h=HEADS, kind=2
+            )
+            for a in range(ROUND_TILES):
+                nc.scalar.copy(
+                    out=heads[:, a, :, KEPT, :],
+                    in_=banks[a, KEPT][:].rearrange("p (h f) -> p h f", h=HEADS),
+                )
+                sums = banks[a, ROTATED][:].rearrange("p (h i e) -> p h i e", h=HEADS, e=2)
+                rotated = heads[:, a, :, ROTATED, :].rearrange("p h (i e) -> p h i e", e=2)
+                where = (r % POSITION_ROUNDS, a)
+                nc.vector.tensor_tensor(
+                    out=rotated,
+                    in0=sums,
+                    in1=cosines[:, where[0], where[1], :, 0:1]
+                    .unsqueeze(1)
+                    .to_broadcast([P, HEADS, PAIRS, 2]),
+                    op=MULT,
+                )
+                cross = cross_pool.tile([P, 2 * HEADS * PAIRS], F32, name="cross")
+                planes = cross[:].rearrange("p (e h i) -> p e h i", e=2, h=HEADS)
+                for e in range(2):
+                    nc.vector.tensor_tensor(
+                        out=planes[:, e],
+                        in0=sums[:, :, :, 1 - e],
+                        in1=signed_sines[:, where[0], where[1], e, :]
+                        .unsqueeze(1)
+                        .to_broadcast([P, HEADS, PAIRS]),
+                        op=MULT,
+                    )
+                nc.gpsimd.tensor_tensor(
+                    out=rotated,
+                    in0=rotated,
+                    in1=cross[:].rearrange("p (e h i) -> p h i e", e=2, h=HEADS),
+                    op=ADD,
+                )
+            nc.sync.dma_start(out=out_rounds[r], in_=out_sb[:])
+
+        for r in range(AHEAD):
+            transpose(r)
+            copy_out(r)
+        for r in range(AHEAD):
+            quantise(r)
+        cosines = table[:].rearrange(
+            "p (r a i two) -> p r a i two", r=POSITION_ROUNDS, a=ROUND_TILES, two=2
+        )
+        sines_sb = keep.tile(
+            [P, POSITION_ROUNDS * ROUND_TILES * 2 * PAIRS], BF16, name="sines_sb"
+        )
+        signed_sines = sines_sb[:].rearrange(
+            "p (r a e i) -> p r a e i", r=POSITION_ROUNDS, a=ROUND_TILES, e=2
+        )
+        for e, sign in ((0, -1.0), (1, 1.0)):
+            nc.vector.tensor_scalar_mul(
+                out=signed_sines[:, :, :, e, :], in0=cosines[:, :, :, :, 1], scalar1=sign
+            )
+
+        for r in range(ROUNDS):
+            if r + AHEAD < ROUNDS:
+                transpose(r + AHEAD)
+                copy_out(r + AHEAD)
+            banks = multiply(r)
+            if r + AHEAD < ROUNDS:
+                quantise(r + AHEAD)
+            finish(r, banks)

@@ -31,6 +31,7 @@ ROUNDS = TOKENS // ROUND_TOKENS
 POSITION_ROUNDS = POSITIONS // ROUND_TOKENS
 AHEAD = 2
 RUN = 4
+VECTOR_HEADS = 2
 
 FLOPS = 2 * TOKENS * K * FEATURES
 
@@ -209,10 +210,17 @@ def tile_multiheadlatentattention_pb_t_kernel(tc, x, freq_cis, Wq, out):
                         .to_broadcast([P, HEADS, PAIRS]),
                         op=MULT,
                     )
+                crossed = cross[:].rearrange("p (e h i) -> p h i e", e=2, h=HEADS)
+                nc.vector.tensor_tensor(
+                    out=rotated[:, :VECTOR_HEADS],
+                    in0=rotated[:, :VECTOR_HEADS],
+                    in1=crossed[:, :VECTOR_HEADS],
+                    op=ADD,
+                )
                 nc.gpsimd.tensor_tensor(
-                    out=rotated,
-                    in0=rotated,
-                    in1=cross[:].rearrange("p (e h i) -> p h i e", e=2, h=HEADS),
+                    out=rotated[:, VECTOR_HEADS:],
+                    in0=rotated[:, VECTOR_HEADS:],
+                    in1=crossed[:, VECTOR_HEADS:],
                     op=ADD,
                 )
             nc.sync.dma_start(out=out_rounds[r], in_=out_sb[:])

@@ -31,7 +31,7 @@ ROUNDS = TOKENS // ROUND_TOKENS
 POSITION_ROUNDS = POSITIONS // ROUND_TOKENS
 AHEAD = 2
 RUN = 4
-VECTOR_HEADS = 2
+VECTOR_HEADS = 1
 
 FLOPS = 2 * TOKENS * K * FEATURES
 
@@ -51,7 +51,7 @@ def tile_multiheadlatentattention_pb_t_kernel(tc, x, freq_cis, Wq, out):
         grouped_pool = ctx.enter_context(tc.tile_pool(name="grouped_pool", bufs=3))
         codes_pool = ctx.enter_context(tc.tile_pool(name="codes_pool", bufs=AHEAD + 2))
         out_pool = ctx.enter_context(tc.tile_pool(name="out_pool", bufs=4))
-        cross_pool = ctx.enter_context(tc.tile_pool(name="cross_pool", bufs=4))
+        cross_pool = ctx.enter_context(tc.tile_pool(name="cross_pool", bufs=3))
         xt_psum = ctx.enter_context(tc.psum_pool(name="xt_psum", bufs=ROUND_TILES))
         kept_psum = ctx.enter_context(tc.psum_pool(name="kept_psum", bufs=3))
         rotated_psum = ctx.enter_context(tc.psum_pool(name="rotated_psum", bufs=3))
@@ -178,52 +178,62 @@ def tile_multiheadlatentattention_pb_t_kernel(tc, x, freq_cis, Wq, out):
                         )
             return banks
 
-        def finish(r, banks):
+        out_tiles = {}
+        cross_tiles = {}
+
+        def products(r, banks):
             out_sb = out_pool.tile([P, ROUND_TILES * FEATURES], F32, name="out_sb")
             heads = out_sb[:].rearrange(
                 "p (a h kind f) -> p a h kind f", a=ROUND_TILES, h=HEADS, kind=2
             )
+            cross = cross_pool.tile([P, 2 * ROUND_TILES * HEADS * PAIRS], F32, name="cross")
+            planes = cross[:].rearrange("p (e a h i) -> p e a h i", e=2, a=ROUND_TILES, h=HEADS)
             for a in range(ROUND_TILES):
                 nc.scalar.copy(
                     out=heads[:, a, :, KEPT, :],
                     in_=banks[a, KEPT][:].rearrange("p (h f) -> p h f", h=HEADS),
                 )
                 sums = banks[a, ROTATED][:].rearrange("p (h i e) -> p h i e", h=HEADS, e=2)
-                rotated = heads[:, a, :, ROTATED, :].rearrange("p h (i e) -> p h i e", e=2)
-                where = (r % POSITION_ROUNDS, a)
                 nc.vector.tensor_tensor(
-                    out=rotated,
+                    out=heads[:, a, :, ROTATED, :].rearrange("p h (i e) -> p h i e", e=2),
                     in0=sums,
-                    in1=cosines[:, where[0], where[1], :, 0:1]
+                    in1=cosines[:, r % POSITION_ROUNDS, a, :, 0:1]
                     .unsqueeze(1)
                     .to_broadcast([P, HEADS, PAIRS, 2]),
                     op=MULT,
                 )
-                cross = cross_pool.tile([P, 2 * HEADS * PAIRS], F32, name="cross")
-                planes = cross[:].rearrange("p (e h i) -> p e h i", e=2, h=HEADS)
                 for e in range(2):
                     nc.vector.tensor_tensor(
-                        out=planes[:, e],
+                        out=planes[:, e, a],
                         in0=sums[:, :, :, 1 - e],
-                        in1=signed_sines[:, where[0], where[1], e, :]
+                        in1=signed_sines[:, r % POSITION_ROUNDS, a, e, :]
                         .unsqueeze(1)
                         .to_broadcast([P, HEADS, PAIRS]),
                         op=MULT,
                     )
-                crossed = cross[:].rearrange("p (e h i) -> p h i e", e=2, h=HEADS)
-                nc.vector.tensor_tensor(
-                    out=rotated[:, :VECTOR_HEADS],
-                    in0=rotated[:, :VECTOR_HEADS],
-                    in1=crossed[:, :VECTOR_HEADS],
-                    op=ADD,
-                )
-                nc.gpsimd.tensor_tensor(
-                    out=rotated[:, VECTOR_HEADS:],
-                    in0=rotated[:, VECTOR_HEADS:],
-                    in1=crossed[:, VECTOR_HEADS:],
-                    op=ADD,
-                )
-            nc.sync.dma_start(out=out_rounds[r], in_=out_sb[:])
+            out_tiles[r] = out_sb
+            cross_tiles[r] = cross
+
+        def add_and_store(r):
+            rotated = out_tiles[r][:].rearrange(
+                "p (a h kind i e) -> p a h kind i e", a=ROUND_TILES, h=HEADS, kind=2, e=2
+            )[:, :, :, ROTATED]
+            crossed = cross_tiles[r][:].rearrange(
+                "p (e a h i) -> p a h i e", e=2, a=ROUND_TILES, h=HEADS
+            )
+            nc.vector.tensor_tensor(
+                out=rotated[:, :, :VECTOR_HEADS],
+                in0=rotated[:, :, :VECTOR_HEADS],
+                in1=crossed[:, :, :VECTOR_HEADS],
+                op=ADD,
+            )
+            nc.gpsimd.tensor_tensor(
+                out=rotated[:, :, VECTOR_HEADS:],
+                in0=rotated[:, :, VECTOR_HEADS:],
+                in1=crossed[:, :, VECTOR_HEADS:],
+                op=ADD,
+            )
+            nc.sync.dma_start(out=out_rounds[r], in_=out_tiles[r][:])
 
         for r in range(AHEAD):
             transpose(r)
@@ -248,7 +258,7 @@ def tile_multiheadlatentattention_pb_t_kernel(tc, x, freq_cis, Wq, out):
             if r + AHEAD < ROUNDS:
                 transpose(r + AHEAD)
                 copy_out(r + AHEAD)
-            banks = multiply(r)
+            products(r, multiply(r))
             if r + AHEAD < ROUNDS:
                 quantise(r + AHEAD)
-            finish(r, banks)
+            add_and_store(r)

@@ -31,7 +31,7 @@ ROUNDS = TOKENS // ROUND_TOKENS
 POSITION_ROUNDS = POSITIONS // ROUND_TOKENS
 AHEAD = 2
 RUN = 4
-VECTOR_HEADS = 1
+VECTOR_PAIRS = 24
 
 FLOPS = 2 * TOKENS * K * FEATURES
 
@@ -222,15 +222,15 @@ def tile_multiheadlatentattention_pb_t_kernel(tc, x, freq_cis, Wq, out):
                 "p (e a h i) -> p a h i e", e=2, a=ROUND_TILES, h=HEADS
             )
             nc.vector.tensor_tensor(
-                out=rotated[:, :, :VECTOR_HEADS],
-                in0=rotated[:, :, :VECTOR_HEADS],
-                in1=crossed[:, :, :VECTOR_HEADS],
+                out=rotated[:, :, :, :VECTOR_PAIRS],
+                in0=rotated[:, :, :, :VECTOR_PAIRS],
+                in1=crossed[:, :, :, :VECTOR_PAIRS],
                 op=ADD,
             )
             nc.gpsimd.tensor_tensor(
-                out=rotated[:, :, VECTOR_HEADS:],
-                in0=rotated[:, :, VECTOR_HEADS:],
-                in1=crossed[:, :, VECTOR_HEADS:],
+                out=rotated[:, :, :, VECTOR_PAIRS:],
+                in0=rotated[:, :, :, VECTOR_PAIRS:],
+                in1=crossed[:, :, :, VECTOR_PAIRS:],
                 op=ADD,
             )
             nc.sync.dma_start(out=out_rounds[r], in_=out_tiles[r][:])

@@ -25,13 +25,14 @@ FEATURES = HEADS * 2 * HALF_HEAD
 BANK = HEADS * HALF_HEAD
 KEPT = 0
 ROTATED = 1
+KINDS = (ROTATED, KEPT)
 ROUND_TILES = 2
 ROUND_TOKENS = ROUND_TILES * P
 ROUNDS = TOKENS // ROUND_TOKENS
-POSITION_ROUNDS = POSITIONS // ROUND_TOKENS
+POSITION_TILES = POSITIONS // P
 AHEAD = 2
 RUN = 4
-VECTOR_PAIRS = 24
+VECTOR_PAIRS = 16
 
 FLOPS = 2 * TOKENS * K * FEATURES
 
@@ -42,7 +43,7 @@ def tile_multiheadlatentattention_pb_t_kernel(tc, x, freq_cis, Wq, out):
         "(r p a) k -> r p (a k)", p=P, a=ROUND_TILES
     )
     out_rounds = out.rearrange("b t h f -> (b t) (h f)").rearrange(
-        "(r p a) f -> r p (a f)", p=P, a=ROUND_TILES
+        "(r p a) f -> r p a f", p=P, a=ROUND_TILES
     )
 
     with ExitStack() as ctx:
@@ -50,45 +51,49 @@ def tile_multiheadlatentattention_pb_t_kernel(tc, x, freq_cis, Wq, out):
         x_pool = ctx.enter_context(tc.tile_pool(name="x_pool", bufs=ROUNDS))
         grouped_pool = ctx.enter_context(tc.tile_pool(name="grouped_pool", bufs=3))
         codes_pool = ctx.enter_context(tc.tile_pool(name="codes_pool", bufs=AHEAD + 2))
-        out_pool = ctx.enter_context(tc.tile_pool(name="out_pool", bufs=4))
+        out_pool = ctx.enter_context(tc.tile_pool(name="out_pool", bufs=6))
         cross_pool = ctx.enter_context(tc.tile_pool(name="cross_pool", bufs=3))
         xt_psum = ctx.enter_context(tc.psum_pool(name="xt_psum", bufs=ROUND_TILES))
         kept_psum = ctx.enter_context(tc.psum_pool(name="kept_psum", bufs=3))
         rotated_psum = ctx.enter_context(tc.psum_pool(name="rotated_psum", bufs=3))
         ctx.enter_context(tc.manual_schedule())
 
-        w_raw = []
-        for g in range(PASSES):
-            w_rows = keep.tile([P, PACK * FEATURES], BF16, name="w_raw%d" % g)
+        table = keep.tile([P, POSITION_TILES * PAIRS * 2], BF16, name="table")
+        nc.sync.dma_start(
+            out=table[:].rearrange("p (r c) -> p r c", c=ROUND_TILES * PAIRS * 2),
+            in_=freq_cis.rearrange("(r p a) i two -> p r (a i two)", p=P, a=ROUND_TILES),
+        )
+        w_raw = {}
+        x_tiles = {}
+
+        def load_weights(g):
+            w_raw[g] = keep.tile([P, PACK * FEATURES], BF16, name="w_raw%d" % g)
             nc.sync.dma_start(
-                out=w_rows[:].rearrange("q (u c) -> q u c", u=2),
+                out=w_raw[g][:].rearrange("q (u c) -> q u c", u=2),
                 in_=Wq[g * K_PASS : (g + 1) * K_PASS, :].rearrange(
                     "(u q e) c -> q u (e c)", u=2, e=2
                 ),
             )
-            w_raw.append(w_rows)
-        table = keep.tile([P, POSITION_ROUNDS * ROUND_TILES * PAIRS * 2], BF16, name="table")
-        x_tiles = []
-        for r in range(ROUNDS):
-            x_sb = x_pool.tile([P, ROUND_TILES * K], BF16, name="x_sb")
-            nc.sync.dma_start(out=x_sb[:], in_=x_rounds[r])
-            x_tiles.append(x_sb)
-            if r == 0:
-                nc.sync.dma_start(
-                    out=table[:].rearrange("p (r c) -> p r c", r=POSITION_ROUNDS),
-                    in_=freq_cis.rearrange(
-                        "(r p a) i two -> p r (a i two)", p=P, a=ROUND_TILES
-                    ),
-                )
+
+        def load_x(r):
+            x_tiles[r] = x_pool.tile([P, ROUND_TILES * K], BF16, name="x_sb")
+            nc.sync.dma_start(out=x_tiles[r][:], in_=x_rounds[r])
+
+        load_weights(0)
+        load_x(0)
+        load_weights(1)
+        for r in range(1, ROUNDS):
+            load_x(r)
 
         identity = keep.tile([P, P], F32, name="identity")
         make_identity(nc, identity[:])
 
+        w_grouped = {}
         w_codes = {}
         w_scales = {}
-        w_grouped = {}
-        for g in range(PASSES):
-            for kind in (KEPT, ROTATED):
+
+        def regroup_weights(g):
+            for kind in KINDS:
                 grouped = keep.tile(
                     [P, BANK * PACK], BF16, name="w_grouped%d%d" % (g, kind), align_bytes=64
                 )
@@ -104,8 +109,9 @@ def tile_multiheadlatentattention_pb_t_kernel(tc, x, freq_cis, Wq, out):
                         nc.vector.tensor_copy(out=words, in_=rows)
                     else:
                         nc.scalar.copy(out=words, in_=rows)
-        for g in range(PASSES):
-            for kind in (KEPT, ROTATED):
+
+        def quantise_weights(g):
+            for kind in KINDS:
                 w_codes[g, kind] = keep.tile(
                     [P, BANK], U32, name="w_codes%d%d" % (g, kind), align_bytes=64
                 )
@@ -122,6 +128,9 @@ def tile_multiheadlatentattention_pb_t_kernel(tc, x, freq_cis, Wq, out):
         x_grouped = {}
         x_codes = {}
         x_scales = {}
+        banks = {}
+        out_tiles = {}
+        cross_tiles = {}
 
         def transpose(r):
             words = x_tiles[r][:].bitcast(F32)
@@ -160,15 +169,17 @@ def tile_multiheadlatentattention_pb_t_kernel(tc, x, freq_cis, Wq, out):
             )
 
         def multiply(r):
-            banks = {}
-            for a in range(ROUND_TILES):
-                banks[a, KEPT] = kept_psum.tile([P, BANK], F32, name="kept")
-                banks[a, ROTATED] = rotated_psum.tile([P, BANK], F32, name="rotated")
-                for kind in (KEPT, ROTATED):
+            for kind in KINDS:
+                for a in range(ROUND_TILES):
+                    if kind == KEPT:
+                        bank = kept_psum.tile([P, BANK], F32, name="kept")
+                    else:
+                        bank = rotated_psum.tile([P, BANK], F32, name="rotated")
+                    banks[r, a, kind] = bank
                     for g in range(PASSES):
                         tokens = slice((a * PASSES + g) * P, (a * PASSES + g + 1) * P)
                         nc.tensor.matmul_mx(
-                            out=banks[a, kind][:],
+                            out=bank[:],
                             lhsT=x_codes[r][:, tokens].bitcast(FP8X4),
                             lhsT_scale=x_scales[r][:, tokens],
                             rhs=w_codes[g, kind][:].bitcast(FP8X4),
@@ -176,89 +187,102 @@ def tile_multiheadlatentattention_pb_t_kernel(tc, x, freq_cis, Wq, out):
                             start=(g == 0),
                             stop=(g == PASSES - 1),
                         )
-            return banks
+            out_tiles[r] = out_pool.tile([P, ROUND_TILES * FEATURES], F32, name="out_sb")
+            cross_tiles[r] = cross_pool.tile([P, ROUND_TILES * BANK], F32, name="cross")
 
-        out_tiles = {}
-        cross_tiles = {}
-
-        def products(r, banks):
-            out_sb = out_pool.tile([P, ROUND_TILES * FEATURES], F32, name="out_sb")
-            heads = out_sb[:].rearrange(
-                "p (a h kind f) -> p a h kind f", a=ROUND_TILES, h=HEADS, kind=2
-            )
-            cross = cross_pool.tile([P, 2 * ROUND_TILES * HEADS * PAIRS], F32, name="cross")
-            planes = cross[:].rearrange("p (e a h i) -> p e a h i", e=2, a=ROUND_TILES, h=HEADS)
-            for a in range(ROUND_TILES):
-                nc.scalar.copy(
-                    out=heads[:, a, :, KEPT, :],
-                    in_=banks[a, KEPT][:].rearrange("p (h f) -> p h f", h=HEADS),
-                )
-                sums = banks[a, ROTATED][:].rearrange("p (h i e) -> p h i e", h=HEADS, e=2)
-                nc.vector.tensor_tensor(
-                    out=heads[:, a, :, ROTATED, :].rearrange("p h (i e) -> p h i e", e=2),
-                    in0=sums,
-                    in1=cosines[:, r % POSITION_ROUNDS, a, :, 0:1]
-                    .unsqueeze(1)
-                    .to_broadcast([P, HEADS, PAIRS, 2]),
-                    op=MULT,
-                )
-                for e in range(2):
-                    nc.vector.tensor_tensor(
-                        out=planes[:, e, a],
-                        in0=sums[:, :, :, 1 - e],
-                        in1=signed_sines[:, r % POSITION_ROUNDS, a, e, :]
-                        .unsqueeze(1)
-                        .to_broadcast([P, HEADS, PAIRS]),
-                        op=MULT,
-                    )
-            out_tiles[r] = out_sb
-            cross_tiles[r] = cross
-
-        def add_and_store(r):
-            rotated = out_tiles[r][:].rearrange(
+        def rotated_part(r):
+            return out_tiles[r][:].rearrange(
                 "p (a h kind i e) -> p a h kind i e", a=ROUND_TILES, h=HEADS, kind=2, e=2
             )[:, :, :, ROTATED]
-            crossed = cross_tiles[r][:].rearrange(
-                "p (e a h i) -> p a h i e", e=2, a=ROUND_TILES, h=HEADS
+
+        def cross_part(r):
+            return cross_tiles[r][:].rearrange(
+                "p (a h i e) -> p a h i e", a=ROUND_TILES, h=HEADS, e=2
             )
+
+        def copy_kept(r):
+            for a in range(ROUND_TILES):
+                nc.scalar.copy(
+                    out=out_tiles[r][:].rearrange(
+                        "p (a h kind f) -> p a h kind f", a=ROUND_TILES, h=HEADS, kind=2
+                    )[:, a, :, KEPT, :],
+                    in_=banks[r, a, KEPT][:].rearrange("p (h f) -> p h f", h=HEADS),
+                )
+
+        def products(r, a):
+            sums = banks[r, a, ROTATED][:].rearrange("p (h i e) -> p h i e", h=HEADS, e=2)
+            where = (r * ROUND_TILES + a) % POSITION_TILES
+            nc.vector.tensor_tensor(
+                out=rotated_part(r)[:, a],
+                in0=sums,
+                in1=cosines[:, where].unsqueeze(1).to_broadcast([P, HEADS, PAIRS, 2]),
+                op=MULT,
+            )
+            nc.vector.tensor_tensor(
+                out=cross_part(r)[:, a],
+                in0=sums[:, :, :, ::-1],
+                in1=signed_sines[:, where].unsqueeze(1).to_broadcast([P, HEADS, PAIRS, 2]),
+                op=MULT,
+            )
+
+        def add_and_store(r, tiles):
+            rotated = rotated_part(r)[:, tiles]
+            cross = cross_part(r)[:, tiles]
             nc.vector.tensor_tensor(
                 out=rotated[:, :, :, :VECTOR_PAIRS],
                 in0=rotated[:, :, :, :VECTOR_PAIRS],
-                in1=crossed[:, :, :, :VECTOR_PAIRS],
+                in1=cross[:, :, :, :VECTOR_PAIRS],
                 op=ADD,
             )
             nc.gpsimd.tensor_tensor(
                 out=rotated[:, :, :, VECTOR_PAIRS:],
                 in0=rotated[:, :, :, VECTOR_PAIRS:],
-                in1=crossed[:, :, :, VECTOR_PAIRS:],
+                in1=cross[:, :, :, VECTOR_PAIRS:],
                 op=ADD,
             )
-            nc.sync.dma_start(out=out_rounds[r], in_=out_tiles[r][:])
-
-        for r in range(AHEAD):
-            transpose(r)
-            copy_out(r)
-        for r in range(AHEAD):
-            quantise(r)
-        cosines = table[:].rearrange(
-            "p (r a i two) -> p r a i two", r=POSITION_ROUNDS, a=ROUND_TILES, two=2
-        )
-        sines_sb = keep.tile(
-            [P, POSITION_ROUNDS * ROUND_TILES * 2 * PAIRS], BF16, name="sines_sb"
-        )
-        signed_sines = sines_sb[:].rearrange(
-            "p (r a e i) -> p r a e i", r=POSITION_ROUNDS, a=ROUND_TILES, e=2
-        )
-        for e, sign in ((0, -1.0), (1, 1.0)):
-            nc.vector.tensor_scalar_mul(
-                out=signed_sines[:, :, :, e, :], in0=cosines[:, :, :, :, 1], scalar1=sign
+            nc.sync.dma_start(
+                out=out_rounds[r][:, tiles],
+                in_=out_tiles[r][:].rearrange("p (a f) -> p a f", a=ROUND_TILES)[:, tiles],
             )
 
+        angles = table[:].rearrange("p (n i two) -> p n i two", n=POSITION_TILES, two=2)
+        cosines = angles[:, :, :, 0:1]
+        signs = keep.tile([P, 2], BF16, name="signs")
+        nc.vector.memset(signs[:, 0:1], -1.0)
+        nc.vector.memset(signs[:, 1:2], 1.0)
+        sines_sb = keep.tile([P, POSITION_TILES * PAIRS * 2], BF16, name="sines_sb")
+        signed_sines = sines_sb[:].rearrange("p (n i e) -> p n i e", n=POSITION_TILES, e=2)
+        nc.vector.tensor_tensor(
+            out=signed_sines,
+            in0=angles[:, :, :, 1:2].to_broadcast([P, POSITION_TILES, PAIRS, 2]),
+            in1=signs[:].unsqueeze(1).unsqueeze(1).to_broadcast([P, POSITION_TILES, PAIRS, 2]),
+            op=MULT,
+        )
+        regroup_weights(0)
+        quantise_weights(0)
+        transpose(0)
+        copy_out(0)
+        regroup_weights(1)
+        quantise(0)
+        quantise_weights(1)
+        transpose(1)
+        copy_out(1)
+
+        next_x = 1
         for r in range(ROUNDS):
+            multiply(r)
+            copy_kept(r)
             if r + AHEAD < ROUNDS:
                 transpose(r + AHEAD)
                 copy_out(r + AHEAD)
-            products(r, multiply(r))
-            if r + AHEAD < ROUNDS:
-                quantise(r + AHEAD)
-            add_and_store(r)
+            if next_x < ROUNDS:
+                for a in range(ROUND_TILES):
+                    products(r, a)
+                while next_x <= min(r + AHEAD, ROUNDS - 1):
+                    quantise(next_x)
+                    next_x += 1
+                add_and_store(r, slice(0, ROUND_TILES))
+            else:
+                for a in range(ROUND_TILES):
+                    products(r, a)
+                    add_and_store(r, slice(a, a + 1))

@@ -31,28 +31,30 @@ ROUND_TOKENS = ROUND_TILES * P
 ROUNDS = TOKENS // ROUND_TOKENS
 POSITION_TILES = POSITIONS // P
 AHEAD = 2
+assert AHEAD == 2
 RUN = 4
 VECTOR_PAIRS = 16
+OUT_TILES = 6
 
 FLOPS = 2 * TOKENS * K * FEATURES
 
 
 def tile_multiheadlatentattention_pb_t_kernel(tc, x, freq_cis, Wq, out):
     nc = tc.nc
-    x_rounds = x.rearrange("b t k -> (b t) k").rearrange(
+    x_rounds = x.rearrange("b pos k -> (b pos) k").rearrange(
         "(r p a) k -> r p (a k)", p=P, a=ROUND_TILES
     )
-    out_rounds = out.rearrange("b t h f -> (b t) (h f)").rearrange(
+    out_rounds = out.rearrange("b pos h f -> (b pos) (h f)").rearrange(
         "(r p a) f -> r p a f", p=P, a=ROUND_TILES
     )
 
     with ExitStack() as ctx:
         keep = ctx.enter_context(tc.tile_pool(name="keep", bufs=1))
         x_pool = ctx.enter_context(tc.tile_pool(name="x_pool", bufs=ROUNDS))
-        grouped_pool = ctx.enter_context(tc.tile_pool(name="grouped_pool", bufs=3))
+        grouped_pool = ctx.enter_context(tc.tile_pool(name="grouped_pool", bufs=AHEAD + 1))
         codes_pool = ctx.enter_context(tc.tile_pool(name="codes_pool", bufs=AHEAD + 2))
-        out_pool = ctx.enter_context(tc.tile_pool(name="out_pool", bufs=6))
-        cross_pool = ctx.enter_context(tc.tile_pool(name="cross_pool", bufs=3))
+        out_pool = ctx.enter_context(tc.tile_pool(name="out_pool", bufs=OUT_TILES))
+        sine_pool = ctx.enter_context(tc.tile_pool(name="sine_pool", bufs=3))
         xt_psum = ctx.enter_context(tc.psum_pool(name="xt_psum", bufs=ROUND_TILES))
         kept_psum = ctx.enter_context(tc.psum_pool(name="kept_psum", bufs=3))
         rotated_psum = ctx.enter_context(tc.psum_pool(name="rotated_psum", bufs=3))
@@ -60,7 +62,7 @@ def tile_multiheadlatentattention_pb_t_kernel(tc, x, freq_cis, Wq, out):
 
         table = keep.tile([P, POSITION_TILES * PAIRS * 2], BF16, name="table")
         nc.sync.dma_start(
-            out=table[:].rearrange("p (r c) -> p r c", c=ROUND_TILES * PAIRS * 2),
+            out=table[:].rearrange("p (r col) -> p r col", col=ROUND_TILES * PAIRS * 2),
             in_=freq_cis.rearrange("(r p a) i two -> p r (a i two)", p=P, a=ROUND_TILES),
         )
         w_raw = {}
@@ -69,9 +71,9 @@ def tile_multiheadlatentattention_pb_t_kernel(tc, x, freq_cis, Wq, out):
         def load_weights(g):
             w_raw[g] = keep.tile([P, PACK * FEATURES], BF16, name="w_raw%d" % g)
             nc.sync.dma_start(
-                out=w_raw[g][:].rearrange("q (u c) -> q u c", u=2),
+                out=w_raw[g][:].rearrange("q (u col) -> q u col", u=2),
                 in_=Wq[g * K_PASS : (g + 1) * K_PASS, :].rearrange(
-                    "(u q e) c -> q u (e c)", u=2, e=2
+                    "(u q e) col -> q u (e col)", u=2, e=2
                 ),
             )
 
@@ -94,21 +96,20 @@ def tile_multiheadlatentattention_pb_t_kernel(tc, x, freq_cis, Wq, out):
 
         def regroup_weights(g):
             for kind in KINDS:
-                grouped = keep.tile(
+                w_grouped[g, kind] = keep.tile(
                     [P, BANK * PACK], BF16, name="w_grouped%d%d" % (g, kind), align_bytes=64
                 )
-                w_grouped[g, kind] = grouped
                 for h in range(HEADS):
                     rows = w_raw[g][:].rearrange(
-                        "q (t h kind c i) -> q h kind c t i", t=PACK, h=HEADS, kind=2, i=RUN
+                        "q (t h kind run col) -> q h kind run t col", t=PACK, h=HEADS, kind=2, col=RUN
                     )[:, h, kind]
-                    words = grouped[:].rearrange(
-                        "q (h c i t) -> q h c t i", h=HEADS, i=RUN, t=PACK
+                    side_by_side = w_grouped[g, kind][:].rearrange(
+                        "q (h run col t) -> q h run t col", h=HEADS, col=RUN, t=PACK
                     )[:, h]
                     if h < HEADS // 2:
-                        nc.vector.tensor_copy(out=words, in_=rows)
+                        nc.vector.tensor_copy(out=side_by_side, in_=rows)
                     else:
-                        nc.scalar.copy(out=words, in_=rows)
+                        nc.scalar.copy(out=side_by_side, in_=rows)
 
         def quantise_weights(g):
             for kind in KINDS:
@@ -130,32 +131,34 @@ def tile_multiheadlatentattention_pb_t_kernel(tc, x, freq_cis, Wq, out):
         x_scales = {}
         banks = {}
         out_tiles = {}
-        cross_tiles = {}
+        sine_tiles = {}
 
         def transpose(r):
             words = x_tiles[r][:].bitcast(F32)
             for a in range(ROUND_TILES):
-                xt = xt_psum.tile([P, PASSES * 2 * P], F32, name="xt")
+                xt_banks[r, a] = xt_psum.tile([P, PASSES * 2 * P], F32, name="xt")
                 for j in range(PASSES * 2):
                     first = (a * PASSES * 2 + j) * P
                     nc.tensor.transpose(
-                        xt[:, j * P : (j + 1) * P], words[:, first : first + P], identity[:]
+                        xt_banks[r, a][:, j * P : (j + 1) * P],
+                        words[:, first : first + P],
+                        identity[:],
                     )
-                xt_banks[r, a] = xt
 
         def copy_out(r):
-            grouped = grouped_pool.tile(
+            x_grouped[r] = grouped_pool.tile(
                 [P, ROUND_TILES * PASSES * P * PACK], BF16, name="x_grouped", align_bytes=64
             )
-            pairs = grouped[:].bitcast(F32).rearrange(
-                "q (a g n u) -> q a g n u", a=ROUND_TILES, g=PASSES, u=2
+            side_by_side = x_grouped[r][:].bitcast(F32).rearrange(
+                "q (a g token u) -> q a g token u", a=ROUND_TILES, g=PASSES, u=2
             )
             for a in range(ROUND_TILES):
                 nc.scalar.copy(
-                    out=pairs[:, a],
-                    in_=xt_banks[r, a][:].rearrange("q (g u n) -> q g n u", g=PASSES, u=2),
+                    out=side_by_side[:, a],
+                    in_=xt_banks[r, a][:].rearrange(
+                        "q (g u token) -> q g token u", g=PASSES, u=2
+                    ),
                 )
-            x_grouped[r] = grouped
 
         def quantise(r):
             x_codes[r] = codes_pool.tile(
@@ -172,14 +175,13 @@ def tile_multiheadlatentattention_pb_t_kernel(tc, x, freq_cis, Wq, out):
             for kind in KINDS:
                 for a in range(ROUND_TILES):
                     if kind == KEPT:
-                        bank = kept_psum.tile([P, BANK], F32, name="kept")
+                        banks[r, a, kind] = kept_psum.tile([P, BANK], F32, name="kept")
                     else:
-                        bank = rotated_psum.tile([P, BANK], F32, name="rotated")
-                    banks[r, a, kind] = bank
+                        banks[r, a, kind] = rotated_psum.tile([P, BANK], F32, name="rotated")
                     for g in range(PASSES):
                         tokens = slice((a * PASSES + g) * P, (a * PASSES + g + 1) * P)
                         nc.tensor.matmul_mx(
-                            out=bank[:],
+                            out=banks[r, a, kind][:],
                             lhsT=x_codes[r][:, tokens].bitcast(FP8X4),
                             lhsT_scale=x_scales[r][:, tokens],
                             rhs=w_codes[g, kind][:].bitcast(FP8X4),
@@ -188,17 +190,7 @@ def tile_multiheadlatentattention_pb_t_kernel(tc, x, freq_cis, Wq, out):
                             stop=(g == PASSES - 1),
                         )
             out_tiles[r] = out_pool.tile([P, ROUND_TILES * FEATURES], F32, name="out_sb")
-            cross_tiles[r] = cross_pool.tile([P, ROUND_TILES * BANK], F32, name="cross")
-
-        def rotated_part(r):
-            return out_tiles[r][:].rearrange(
-                "p (a h kind i e) -> p a h kind i e", a=ROUND_TILES, h=HEADS, kind=2, e=2
-            )[:, :, :, ROTATED]
-
-        def cross_part(r):
-            return cross_tiles[r][:].rearrange(
-                "p (a h i e) -> p a h i e", a=ROUND_TILES, h=HEADS, e=2
-            )
+            sine_tiles[r] = sine_pool.tile([P, ROUND_TILES * BANK], F32, name="sine_terms")
 
         def copy_kept(r):
             for a in range(ROUND_TILES):
@@ -209,35 +201,53 @@ def tile_multiheadlatentattention_pb_t_kernel(tc, x, freq_cis, Wq, out):
                     in_=banks[r, a, KEPT][:].rearrange("p (h f) -> p h f", h=HEADS),
                 )
 
+        def cosine_terms(r):
+            return out_tiles[r][:].rearrange(
+                "p (a h kind i member) -> p a h kind i member",
+                a=ROUND_TILES,
+                h=HEADS,
+                kind=2,
+                member=2,
+            )[:, :, :, ROTATED]
+
+        def sine_terms(r):
+            return sine_tiles[r][:].rearrange(
+                "p (a h i member) -> p a h i member", a=ROUND_TILES, h=HEADS, member=2
+            )
+
         def products(r, a):
-            sums = banks[r, a, ROTATED][:].rearrange("p (h i e) -> p h i e", h=HEADS, e=2)
-            where = (r * ROUND_TILES + a) % POSITION_TILES
+            y = banks[r, a, ROTATED][:].rearrange(
+                "p (h i member) -> p h i member", h=HEADS, member=2
+            )
+            position_tile = (r * ROUND_TILES + a) % POSITION_TILES
             nc.vector.tensor_tensor(
-                out=rotated_part(r)[:, a],
-                in0=sums,
-                in1=cosines[:, where].unsqueeze(1).to_broadcast([P, HEADS, PAIRS, 2]),
+                out=cosine_terms(r)[:, a],
+                in0=y,
+                in1=cosines[:, position_tile].unsqueeze(1).to_broadcast([P, HEADS, PAIRS, 2]),
                 op=MULT,
             )
             nc.vector.tensor_tensor(
-                out=cross_part(r)[:, a],
-                in0=sums[:, :, :, ::-1],
-                in1=signed_sines[:, where].unsqueeze(1).to_broadcast([P, HEADS, PAIRS, 2]),
+                out=sine_terms(r)[:, a],
+                in0=y[:, :, :, ::-1],
+                in1=signed_sines[:, position_tile]
+                .unsqueeze(1)
+                .to_broadcast([P, HEADS, PAIRS, 2]),
                 op=MULT,
             )
 
         def add_and_store(r, tiles):
-            rotated = rotated_part(r)[:, tiles]
-            cross = cross_part(r)[:, tiles]
+            total = cosine_terms(r)[:, tiles]
+            other = sine_terms(r)[:, tiles]
             nc.vector.tensor_tensor(
-                out=rotated[:, :, :, :VECTOR_PAIRS],
-                in0=rotated[:, :, :, :VECTOR_PAIRS],
-                in1=cross[:, :, :, :VECTOR_PAIRS],
+                out=total[:, :, :, :VECTOR_PAIRS],
+                in0=total[:, :, :, :VECTOR_PAIRS],
+                in1=other[:, :, :, :VECTOR_PAIRS],
                 op=ADD,
             )
             nc.gpsimd.tensor_tensor(
-                out=rotated[:, :, :, VECTOR_PAIRS:],
-                in0=rotated[:, :, :, VECTOR_PAIRS:],
-                in1=cross[:, :, :, VECTOR_PAIRS:],
+                out=total[:, :, :, VECTOR_PAIRS:],
+                in0=total[:, :, :, VECTOR_PAIRS:],
+                in1=other[:, :, :, VECTOR_PAIRS:],
                 op=ADD,
             )
             nc.sync.dma_start(
@@ -245,19 +255,22 @@ def tile_multiheadlatentattention_pb_t_kernel(tc, x, freq_cis, Wq, out):
                 in_=out_tiles[r][:].rearrange("p (a f) -> p a f", a=ROUND_TILES)[:, tiles],
             )
 
-        angles = table[:].rearrange("p (n i two) -> p n i two", n=POSITION_TILES, two=2)
+        angles = table[:].rearrange("p (tile i two) -> p tile i two", tile=POSITION_TILES, two=2)
         cosines = angles[:, :, :, 0:1]
         signs = keep.tile([P, 2], BF16, name="signs")
         nc.vector.memset(signs[:, 0:1], -1.0)
         nc.vector.memset(signs[:, 1:2], 1.0)
         sines_sb = keep.tile([P, POSITION_TILES * PAIRS * 2], BF16, name="sines_sb")
-        signed_sines = sines_sb[:].rearrange("p (n i e) -> p n i e", n=POSITION_TILES, e=2)
+        signed_sines = sines_sb[:].rearrange(
+            "p (tile i member) -> p tile i member", tile=POSITION_TILES, member=2
+        )
         nc.vector.tensor_tensor(
             out=signed_sines,
             in0=angles[:, :, :, 1:2].to_broadcast([P, POSITION_TILES, PAIRS, 2]),
             in1=signs[:].unsqueeze(1).unsqueeze(1).to_broadcast([P, POSITION_TILES, PAIRS, 2]),
             op=MULT,
         )
+
         regroup_weights(0)
         quantise_weights(0)
         transpose(0)
@@ -267,20 +280,17 @@ def tile_multiheadlatentattention_pb_t_kernel(tc, x, freq_cis, Wq, out):
         quantise_weights(1)
         transpose(1)
         copy_out(1)
+        quantise(1)
 
-        next_x = 1
         for r in range(ROUNDS):
             multiply(r)
             copy_kept(r)
             if r + AHEAD < ROUNDS:
                 transpose(r + AHEAD)
                 copy_out(r + AHEAD)
-            if next_x < ROUNDS:
                 for a in range(ROUND_TILES):
                     products(r, a)
-                while next_x <= min(r + AHEAD, ROUNDS - 1):
-                    quantise(next_x)
-                    next_x += 1
+                quantise(r + AHEAD)
                 add_and_store(r, slice(0, ROUND_TILES))
             else:
                 for a in range(ROUND_TILES):

@@ -33,7 +33,7 @@ POSITION_TILES = POSITIONS // P
 AHEAD = 2
 assert AHEAD == 2
 RUN = 4
-VECTOR_PAIRS = 16
+VECTOR_PAIRS = 8
 OUT_TILES = 6
 
 FLOPS = 2 * TOKENS * K * FEATURES

@@ -32,6 +32,7 @@ ROUNDS = TOKENS // ROUND_TOKENS
 POSITION_TILES = POSITIONS // P
 AHEAD = 2
 assert AHEAD == 2
+TURN_AHEAD = AHEAD + 1
 RUN = 4
 VECTOR_PAIRS = 8
 OUT_TILES = 6
@@ -282,12 +283,15 @@ def tile_multiheadlatentattention_pb_t_kernel(tc, x, freq_cis, Wq, out):
         copy_out(1)
         quantise(1)
 
+        turned = AHEAD
         for r in range(ROUNDS):
             multiply(r)
             copy_kept(r)
+            while turned <= min(r + TURN_AHEAD, ROUNDS - 1):
+                transpose(turned)
+                copy_out(turned)
+                turned += 1
             if r + AHEAD < ROUNDS:
-                transpose(r + AHEAD)
-                copy_out(r + AHEAD)
                 for a in range(ROUND_TILES):
                     products(r, a)
                 quantise(r + AHEAD)

@@ -33,6 +33,8 @@ POSITION_TILES = POSITIONS // P
 AHEAD = 2
 assert AHEAD == 2
 TURN_AHEAD = AHEAD + 1
+TURN_ROUNDS = 2
+PSUM_BANKS = 8
 RUN = 4
 VECTOR_PAIRS = 8
 OUT_TILES = 6
@@ -52,13 +54,11 @@ def tile_multiheadlatentattention_pb_t_kernel(tc, x, freq_cis, Wq, out):
     with ExitStack() as ctx:
         keep = ctx.enter_context(tc.tile_pool(name="keep", bufs=1))
         x_pool = ctx.enter_context(tc.tile_pool(name="x_pool", bufs=ROUNDS))
-        grouped_pool = ctx.enter_context(tc.tile_pool(name="grouped_pool", bufs=AHEAD + 1))
+        grouped_pool = ctx.enter_context(tc.tile_pool(name="grouped_pool", bufs=TURN_AHEAD + TURN_ROUNDS))
         codes_pool = ctx.enter_context(tc.tile_pool(name="codes_pool", bufs=AHEAD + 2))
         out_pool = ctx.enter_context(tc.tile_pool(name="out_pool", bufs=OUT_TILES))
         sine_pool = ctx.enter_context(tc.tile_pool(name="sine_pool", bufs=3))
-        xt_psum = ctx.enter_context(tc.psum_pool(name="xt_psum", bufs=ROUND_TILES))
-        kept_psum = ctx.enter_context(tc.psum_pool(name="kept_psum", bufs=3))
-        rotated_psum = ctx.enter_context(tc.psum_pool(name="rotated_psum", bufs=3))
+        psum = ctx.enter_context(tc.psum_pool(name="psum", bufs=PSUM_BANKS))
         ctx.enter_context(tc.manual_schedule())
 
         table = keep.tile([P, POSITION_TILES * PAIRS * 2], BF16, name="table")
@@ -137,7 +137,7 @@ def tile_multiheadlatentattention_pb_t_kernel(tc, x, freq_cis, Wq, out):
         def transpose(r):
             words = x_tiles[r][:].bitcast(F32)
             for a in range(ROUND_TILES):
-                xt_banks[r, a] = xt_psum.tile([P, PASSES * 2 * P], F32, name="xt")
+                xt_banks[r, a] = psum.tile([P, BANK], F32, name="bank")
                 for j in range(PASSES * 2):
                     first = (a * PASSES * 2 + j) * P
                     nc.tensor.transpose(
@@ -175,10 +175,7 @@ def tile_multiheadlatentattention_pb_t_kernel(tc, x, freq_cis, Wq, out):
         def multiply(r):
             for kind in KINDS:
                 for a in range(ROUND_TILES):
-                    if kind == KEPT:
-                        banks[r, a, kind] = kept_psum.tile([P, BANK], F32, name="kept")
-                    else:
-                        banks[r, a, kind] = rotated_psum.tile([P, BANK], F32, name="rotated")
+                    banks[r, a, kind] = psum.tile([P, BANK], F32, name="bank")
                     for g in range(PASSES):
                         tokens = slice((a * PASSES + g) * P, (a * PASSES + g + 1) * P)
                         nc.tensor.matmul_mx(
@@ -287,10 +284,13 @@ def tile_multiheadlatentattention_pb_t_kernel(tc, x, freq_cis, Wq, out):
         for r in range(ROUNDS):
             multiply(r)
             copy_kept(r)
-            while turned <= min(r + TURN_AHEAD, ROUNDS - 1):
-                transpose(turned)
-                copy_out(turned)
-                turned += 1
+            if turned <= min(r + TURN_AHEAD, ROUNDS - 1):
+                run = range(turned, min(turned + TURN_ROUNDS, ROUNDS))
+                for later in run:
+                    transpose(later)
+                for later in run:
+                    copy_out(later)
+                turned = run.stop
             if r + AHEAD < ROUNDS:
                 for a in range(ROUND_TILES):
                     products(r, a)

@@ -35,6 +35,7 @@ assert AHEAD == 2
 TURN_AHEAD = AHEAD + 1
 TURN_ROUNDS = 2
 PSUM_BANKS = 8
+HEAD_ROUNDS = 3
 RUN = 4
 VECTOR_PAIRS = 8
 OUT_TILES = 6
@@ -61,11 +62,6 @@ def tile_multiheadlatentattention_pb_t_kernel(tc, x, freq_cis, Wq, out):
         psum = ctx.enter_context(tc.psum_pool(name="psum", bufs=PSUM_BANKS))
         ctx.enter_context(tc.manual_schedule())
 
-        table = keep.tile([P, POSITION_TILES * PAIRS * 2], BF16, name="table")
-        nc.sync.dma_start(
-            out=table[:].rearrange("p (r col) -> p r col", col=ROUND_TILES * PAIRS * 2),
-            in_=freq_cis.rearrange("(r p a) i two -> p r (a i two)", p=P, a=ROUND_TILES),
-        )
         w_raw = {}
         x_tiles = {}
 
@@ -82,10 +78,17 @@ def tile_multiheadlatentattention_pb_t_kernel(tc, x, freq_cis, Wq, out):
             x_tiles[r] = x_pool.tile([P, ROUND_TILES * K], BF16, name="x_sb")
             nc.sync.dma_start(out=x_tiles[r][:], in_=x_rounds[r])
 
-        load_weights(0)
         load_x(0)
+        load_weights(0)
         load_weights(1)
-        for r in range(1, ROUNDS):
+        for r in range(1, HEAD_ROUNDS):
+            load_x(r)
+        table = keep.tile([P, POSITION_TILES * PAIRS * 2], BF16, name="table")
+        nc.sync.dma_start(
+            out=table[:].rearrange("p (r col) -> p r col", col=ROUND_TILES * PAIRS * 2),
+            in_=freq_cis.rearrange("(r p a) i two -> p r (a i two)", p=P, a=ROUND_TILES),
+        )
+        for r in range(HEAD_ROUNDS, ROUNDS):
             load_x(r)
 
         identity = keep.tile([P, P], F32, name="identity")
@@ -262,25 +265,31 @@ def tile_multiheadlatentattention_pb_t_kernel(tc, x, freq_cis, Wq, out):
         signed_sines = sines_sb[:].rearrange(
             "p (tile i member) -> p tile i member", tile=POSITION_TILES, member=2
         )
-        nc.vector.tensor_tensor(
-            out=signed_sines,
-            in0=angles[:, :, :, 1:2].to_broadcast([P, POSITION_TILES, PAIRS, 2]),
-            in1=signs[:].unsqueeze(1).unsqueeze(1).to_broadcast([P, POSITION_TILES, PAIRS, 2]),
-            op=MULT,
-        )
 
-        regroup_weights(0)
-        quantise_weights(0)
+        def build_signed_sines():
+            nc.vector.tensor_tensor(
+                out=signed_sines,
+                in0=angles[:, :, :, 1:2].to_broadcast([P, POSITION_TILES, PAIRS, 2]),
+                in1=signs[:].unsqueeze(1).unsqueeze(1).to_broadcast([P, POSITION_TILES, PAIRS, 2]),
+                op=MULT,
+            )
+
         transpose(0)
         copy_out(0)
-        regroup_weights(1)
         quantise(0)
+        regroup_weights(0)
+        quantise_weights(0)
+        regroup_weights(1)
+        for r in range(1, HEAD_ROUNDS):
+            transpose(r)
         quantise_weights(1)
-        transpose(1)
+        build_signed_sines()
         copy_out(1)
         quantise(1)
+        for r in range(AHEAD, HEAD_ROUNDS):
+            copy_out(r)
 
-        turned = AHEAD
+        turned = HEAD_ROUNDS
         for r in range(ROUNDS):
             multiply(r)
             copy_kept(r)

@@ -35,6 +35,7 @@ assert AHEAD == 2
 TURN_AHEAD = AHEAD + 1
 TURN_ROUNDS = 2
 PSUM_BANKS = 8
+LAST_PARTS = 2
 HEAD_ROUNDS = 3
 RUN = 4
 VECTOR_PAIRS = 8
@@ -216,7 +217,7 @@ def tile_multiheadlatentattention_pb_t_kernel(tc, x, freq_cis, Wq, out):
                 "p (a h i member) -> p a h i member", a=ROUND_TILES, h=HEADS, member=2
             )
 
-        def products(r, a):
+        def products(r, a, sine_parts):
             y = banks[r, a, ROTATED][:].rearrange(
                 "p (h i member) -> p h i member", h=HEADS, member=2
             )
@@ -227,14 +228,33 @@ def tile_multiheadlatentattention_pb_t_kernel(tc, x, freq_cis, Wq, out):
                 in1=cosines[:, position_tile].unsqueeze(1).to_broadcast([P, HEADS, PAIRS, 2]),
                 op=MULT,
             )
-            nc.vector.tensor_tensor(
-                out=sine_terms(r)[:, a],
-                in0=y[:, :, :, ::-1],
-                in1=signed_sines[:, position_tile]
-                .unsqueeze(1)
-                .to_broadcast([P, HEADS, PAIRS, 2]),
-                op=MULT,
-            )
+            part = HEADS // sine_parts
+            for first in range(0, HEADS, part):
+                nc.vector.tensor_tensor(
+                    out=sine_terms(r)[:, a, first : first + part],
+                    in0=y[:, first : first + part, :, ::-1],
+                    in1=signed_sines[:, position_tile]
+                    .unsqueeze(1)
+                    .to_broadcast([P, part, PAIRS, 2]),
+                    op=MULT,
+                )
+
+        def add_last_and_store(r, a, parts):
+            part = HEADS // parts
+            for first in range(0, HEADS, part):
+                heads = slice(first, first + part)
+                nc.vector.tensor_tensor(
+                    out=cosine_terms(r)[:, a, heads],
+                    in0=cosine_terms(r)[:, a, heads],
+                    in1=sine_terms(r)[:, a, heads],
+                    op=ADD,
+                )
+                nc.sync.dma_start(
+                    out=out_rounds[r][:, a].rearrange("p (h f) -> p h f", h=HEADS)[:, heads],
+                    in_=out_tiles[r][:].rearrange(
+                        "p (a h f) -> p a h f", a=ROUND_TILES, h=HEADS
+                    )[:, a, heads],
+                )
 
         def add_and_store(r, tiles):
             total = cosine_terms(r)[:, tiles]
@@ -302,10 +322,14 @@ def tile_multiheadlatentattention_pb_t_kernel(tc, x, freq_cis, Wq, out):
                 turned = run.stop
             if r + AHEAD < ROUNDS:
                 for a in range(ROUND_TILES):
-                    products(r, a)
+                    products(r, a, 1)
                 quantise(r + AHEAD)
                 add_and_store(r, slice(0, ROUND_TILES))
             else:
                 for a in range(ROUND_TILES):
-                    products(r, a)
-                    add_and_store(r, slice(a, a + 1))
+                    if (r, a) == (ROUNDS - 1, ROUND_TILES - 1):
+                        products(r, a, LAST_PARTS)
+                        add_last_and_store(r, a, LAST_PARTS)
+                    else:
+                        products(r, a, 1)
+                        add_and_store(r, slice(a, a + 1))

from contextlib import ExitStack

import concourse.mybir as mybir
from concourse.masks import make_identity

F32 = mybir.dt.float32
BF16 = mybir.dt.bfloat16
U32 = mybir.dt.uint32
U8 = mybir.dt.uint8
FP8X4 = mybir.dt.float8_e4m3fn_x4
MULT = mybir.AluOpType.mult
ADD = mybir.AluOpType.add

P = 128
PACK = 4
K_PASS = P * PACK
TOKENS = 4 * 1024
POSITIONS = 1024
K = 1024
PASSES = K // K_PASS
HEADS = 4
HALF_HEAD = 128
PAIRS = HALF_HEAD // 2
FEATURES = HEADS * 2 * HALF_HEAD
BANK = HEADS * HALF_HEAD
KEPT = 0
ROTATED = 1
KINDS = (ROTATED, KEPT)
ROUND_TILES = 2
ROUND_TOKENS = ROUND_TILES * P
ROUNDS = TOKENS // ROUND_TOKENS
POSITION_TILES = POSITIONS // P
AHEAD = 2
assert AHEAD == 2
TURN_AHEAD = AHEAD + 1
TURN_ROUNDS = 2
PSUM_BANKS = 8
LAST_PARTS = 2
HEAD_ROUNDS = 3
RUN = 4
VECTOR_PAIRS = 8
OUT_TILES = 6

FLOPS = 2 * TOKENS * K * FEATURES


def tile_multiheadlatentattention_pb_t_kernel(tc, x, freq_cis, Wq, out):
    nc = tc.nc
    x_rounds = x.rearrange("b pos k -> (b pos) k").rearrange(
        "(r p a) k -> r p (a k)", p=P, a=ROUND_TILES
    )
    out_rounds = out.rearrange("b pos h f -> (b pos) (h f)").rearrange(
        "(r p a) f -> r p a f", p=P, a=ROUND_TILES
    )

    with ExitStack() as ctx:
        keep = ctx.enter_context(tc.tile_pool(name="keep", bufs=1))
        x_pool = ctx.enter_context(tc.tile_pool(name="x_pool", bufs=ROUNDS))
        grouped_pool = ctx.enter_context(tc.tile_pool(name="grouped_pool", bufs=TURN_AHEAD + TURN_ROUNDS))
        codes_pool = ctx.enter_context(tc.tile_pool(name="codes_pool", bufs=AHEAD + 2))
        out_pool = ctx.enter_context(tc.tile_pool(name="out_pool", bufs=OUT_TILES))
        sine_pool = ctx.enter_context(tc.tile_pool(name="sine_pool", bufs=3))
        psum = ctx.enter_context(tc.psum_pool(name="psum", bufs=PSUM_BANKS))
        ctx.enter_context(tc.manual_schedule())

        w_raw = {}
        x_tiles = {}

        def load_weights(g):
            w_raw[g] = keep.tile([P, PACK * FEATURES], BF16, name="w_raw%d" % g)
            nc.sync.dma_start(
                out=w_raw[g][:].rearrange("q (u col) -> q u col", u=2),
                in_=Wq[g * K_PASS : (g + 1) * K_PASS, :].rearrange(
                    "(u q e) col -> q u (e col)", u=2, e=2
                ),
            )

        def load_x(r):
            x_tiles[r] = x_pool.tile([P, ROUND_TILES * K], BF16, name="x_sb")
            nc.sync.dma_start(out=x_tiles[r][:], in_=x_rounds[r])

        load_x(0)
        load_weights(0)
        load_weights(1)
        for r in range(1, HEAD_ROUNDS):
            load_x(r)
        table = keep.tile([P, POSITION_TILES * PAIRS * 2], BF16, name="table")
        nc.sync.dma_start(
            out=table[:].rearrange("p (r col) -> p r col", col=ROUND_TILES * PAIRS * 2),
            in_=freq_cis.rearrange("(r p a) i two -> p r (a i two)", p=P, a=ROUND_TILES),
        )
        for r in range(HEAD_ROUNDS, ROUNDS):
            load_x(r)

        identity = keep.tile([P, P], F32, name="identity")
        make_identity(nc, identity[:])

        w_grouped = {}
        w_codes = {}
        w_scales = {}

        def regroup_weights(g):
            for kind in KINDS:
                w_grouped[g, kind] = keep.tile(
                    [P, BANK * PACK], BF16, name="w_grouped%d%d" % (g, kind), align_bytes=64
                )
                for h in range(HEADS):
                    rows = w_raw[g][:].rearrange(
                        "q (t h kind run col) -> q h kind run t col", t=PACK, h=HEADS, kind=2, col=RUN
                    )[:, h, kind]
                    side_by_side = w_grouped[g, kind][:].rearrange(
                        "q (h run col t) -> q h run t col", h=HEADS, col=RUN, t=PACK
                    )[:, h]
                    if h < HEADS // 2:
                        nc.vector.tensor_copy(out=side_by_side, in_=rows)
                    else:
                        nc.scalar.copy(out=side_by_side, in_=rows)

        def quantise_weights(g):
            for kind in KINDS:
                w_codes[g, kind] = keep.tile(
                    [P, BANK], U32, name="w_codes%d%d" % (g, kind), align_bytes=64
                )
                w_scales[g, kind] = keep.tile(
                    [P, BANK], U8, name="w_scales%d%d" % (g, kind), align_bytes=64
                )
                nc.vector.quantize_mx(
                    out=w_codes[g, kind][:].bitcast(FP8X4),
                    scales=w_scales[g, kind][:],
                    in_=w_grouped[g, kind][:],
                )

        xt_banks = {}
        x_grouped = {}
        x_codes = {}
        x_scales = {}
        banks = {}
        out_tiles = {}
        sine_tiles = {}

        def transpose(r):
            words = x_tiles[r][:].bitcast(F32)
            for a in range(ROUND_TILES):
                xt_banks[r, a] = psum.tile([P, BANK], F32, name="bank")
                for j in range(PASSES * 2):
                    first = (a * PASSES * 2 + j) * P
                    nc.tensor.transpose(
                        xt_banks[r, a][:, j * P : (j + 1) * P],
                        words[:, first : first + P],
                        identity[:],
                    )

        def copy_out(r):
            x_grouped[r] = grouped_pool.tile(
                [P, ROUND_TILES * PASSES * P * PACK], BF16, name="x_grouped", align_bytes=64
            )
            side_by_side = x_grouped[r][:].bitcast(F32).rearrange(
                "q (a g token u) -> q a g token u", a=ROUND_TILES, g=PASSES, u=2
            )
            for a in range(ROUND_TILES):
                nc.scalar.copy(
                    out=side_by_side[:, a],
                    in_=xt_banks[r, a][:].rearrange(
                        "q (g u token) -> q g token u", g=PASSES, u=2
                    ),
                )

        def quantise(r):
            x_codes[r] = codes_pool.tile(
                [P, ROUND_TILES * PASSES * P], U32, name="x_codes", align_bytes=64
            )
            x_scales[r] = codes_pool.tile(
                [P, ROUND_TILES * PASSES * P], U8, name="x_scales", align_bytes=64
            )
            nc.vector.quantize_mx(
                out=x_codes[r][:].bitcast(FP8X4), scales=x_scales[r][:], in_=x_grouped[r][:]
            )

        def multiply(r):
            for kind in KINDS:
                for a in range(ROUND_TILES):
                    banks[r, a, kind] = psum.tile([P, BANK], F32, name="bank")
                    for g in range(PASSES):
                        tokens = slice((a * PASSES + g) * P, (a * PASSES + g + 1) * P)
                        nc.tensor.matmul_mx(
                            out=banks[r, a, kind][:],
                            lhsT=x_codes[r][:, tokens].bitcast(FP8X4),
                            lhsT_scale=x_scales[r][:, tokens],
                            rhs=w_codes[g, kind][:].bitcast(FP8X4),
                            rhs_scale=w_scales[g, kind][:],
                            start=(g == 0),
                            stop=(g == PASSES - 1),
                        )
            out_tiles[r] = out_pool.tile([P, ROUND_TILES * FEATURES], F32, name="out_sb")
            sine_tiles[r] = sine_pool.tile([P, ROUND_TILES * BANK], F32, name="sine_terms")

        def copy_kept(r):
            for a in range(ROUND_TILES):
                nc.scalar.copy(
                    out=out_tiles[r][:].rearrange(
                        "p (a h kind f) -> p a h kind f", a=ROUND_TILES, h=HEADS, kind=2
                    )[:, a, :, KEPT, :],
                    in_=banks[r, a, KEPT][:].rearrange("p (h f) -> p h f", h=HEADS),
                )

        def cosine_terms(r):
            return out_tiles[r][:].rearrange(
                "p (a h kind i member) -> p a h kind i member",
                a=ROUND_TILES,
                h=HEADS,
                kind=2,
                member=2,
            )[:, :, :, ROTATED]

        def sine_terms(r):
            return sine_tiles[r][:].rearrange(
                "p (a h i member) -> p a h i member", a=ROUND_TILES, h=HEADS, member=2
            )

        def products(r, a, sine_parts):
            y = banks[r, a, ROTATED][:].rearrange(
                "p (h i member) -> p h i member", h=HEADS, member=2
            )
            position_tile = (r * ROUND_TILES + a) % POSITION_TILES
            nc.vector.tensor_tensor(
                out=cosine_terms(r)[:, a],
                in0=y,
                in1=cosines[:, position_tile].unsqueeze(1).to_broadcast([P, HEADS, PAIRS, 2]),
                op=MULT,
            )
            part = HEADS // sine_parts
            for first in range(0, HEADS, part):
                nc.vector.tensor_tensor(
                    out=sine_terms(r)[:, a, first : first + part],
                    in0=y[:, first : first + part, :, ::-1],
                    in1=signed_sines[:, position_tile]
                    .unsqueeze(1)
                    .to_broadcast([P, part, PAIRS, 2]),
                    op=MULT,
                )

        def add_last_and_store(r, a, parts):
            part = HEADS // parts
            for first in range(0, HEADS, part):
                heads = slice(first, first + part)
                nc.vector.tensor_tensor(
                    out=cosine_terms(r)[:, a, heads],
                    in0=cosine_terms(r)[:, a, heads],
                    in1=sine_terms(r)[:, a, heads],
                    op=ADD,
                )
                nc.sync.dma_start(
                    out=out_rounds[r][:, a].rearrange("p (h f) -> p h f", h=HEADS)[:, heads],
                    in_=out_tiles[r][:].rearrange(
                        "p (a h f) -> p a h f", a=ROUND_TILES, h=HEADS
                    )[:, a, heads],
                )

        def add_and_store(r, tiles):
            total = cosine_terms(r)[:, tiles]
            other = sine_terms(r)[:, tiles]
            nc.vector.tensor_tensor(
                out=total[:, :, :, :VECTOR_PAIRS],
                in0=total[:, :, :, :VECTOR_PAIRS],
                in1=other[:, :, :, :VECTOR_PAIRS],
                op=ADD,
            )
            nc.gpsimd.tensor_tensor(
                out=total[:, :, :, VECTOR_PAIRS:],
                in0=total[:, :, :, VECTOR_PAIRS:],
                in1=other[:, :, :, VECTOR_PAIRS:],
                op=ADD,
            )
            nc.sync.dma_start(
                out=out_rounds[r][:, tiles],
                in_=out_tiles[r][:].rearrange("p (a f) -> p a f", a=ROUND_TILES)[:, tiles],
            )

        angles = table[:].rearrange("p (tile i two) -> p tile i two", tile=POSITION_TILES, two=2)
        cosines = angles[:, :, :, 0:1]
        signs = keep.tile([P, 2], BF16, name="signs")
        nc.vector.memset(signs[:, 0:1], -1.0)
        nc.vector.memset(signs[:, 1:2], 1.0)
        sines_sb = keep.tile([P, POSITION_TILES * PAIRS * 2], BF16, name="sines_sb")
        signed_sines = sines_sb[:].rearrange(
            "p (tile i member) -> p tile i member", tile=POSITION_TILES, member=2
        )

        def build_signed_sines():
            nc.vector.tensor_tensor(
                out=signed_sines,
                in0=angles[:, :, :, 1:2].to_broadcast([P, POSITION_TILES, PAIRS, 2]),
                in1=signs[:].unsqueeze(1).unsqueeze(1).to_broadcast([P, POSITION_TILES, PAIRS, 2]),
                op=MULT,
            )

        transpose(0)
        copy_out(0)
        quantise(0)
        regroup_weights(0)
        quantise_weights(0)
        regroup_weights(1)
        for r in range(1, HEAD_ROUNDS):
            transpose(r)
        quantise_weights(1)
        build_signed_sines()
        copy_out(1)
        quantise(1)
        for r in range(AHEAD, HEAD_ROUNDS):
            copy_out(r)

        turned = HEAD_ROUNDS
        for r in range(ROUNDS):
            multiply(r)
            copy_kept(r)
            if turned <= min(r + TURN_AHEAD, ROUNDS - 1):
                run = range(turned, min(turned + TURN_ROUNDS, ROUNDS))
                for later in run:
                    transpose(later)
                for later in run:
                    copy_out(later)
                turned = run.stop
            if r + AHEAD < ROUNDS:
                for a in range(ROUND_TILES):
                    products(r, a, 1)
                quantise(r + AHEAD)
                add_and_store(r, slice(0, ROUND_TILES))
            else:
                for a in range(ROUND_TILES):
                    if (r, a) == (ROUNDS - 1, ROUND_TILES - 1):
                        products(r, a, LAST_PARTS)
                        add_last_and_store(r, a, LAST_PARTS)
                    else:
                        products(r, a, 1)
                        add_and_store(r, slice(a, a + 1))
